import numpy as np
import ml_dtypes


def mxq(x, axis, fmt="e4m3"):
    dtype, down = {"e4m3": (ml_dtypes.float8_e4m3fn, 7), "e5m2": (ml_dtypes.float8_e5m2, 14)}[fmt]
    v = np.moveaxis(np.asarray(x, np.float32).astype(ml_dtypes.bfloat16).astype(np.float64), axis, -1)
    blocks = v.reshape(v.shape[:-1] + (-1, 32))
    amax = np.abs(blocks).max(-1, keepdims=True)
    byte = np.maximum(np.where(amax > 0, np.frexp(amax)[1] - 1 + 127, 0) - down, 1)
    scale = np.exp2(byte - 127.0)
    codes = (blocks / scale).astype(np.float32).astype(dtype).astype(np.float64)
    return np.moveaxis((codes * scale).reshape(v.shape), -1, axis)


WIDE = False


def mx_kscale(k):
    if not WIDE:
        return np.ones(k)
    levels = np.array([10, -10, 5, -5, 0])
    a = np.random.permutation(np.resize(levels, k // 512 * 4)).reshape(k // 512, 4)
    idx = np.arange(k)
    return np.exp2(a[idx // 512, idx % 128 // 32])


BF16 = ml_dtypes.bfloat16


def bf(x):
    return np.asarray(x, np.float32).astype(BF16)


def f64(x):
    return np.asarray(x).astype(np.float64)


E2M1 = np.array([0.0, 0.5, 1.0, 1.5, 2.0, 3.0, 4.0, 6.0, -0.0, -0.5, -1.0, -1.5, -2.0, -3.0, -4.0, -6.0])


def pack_weight(w, fmt):
    k, n = w.shape
    w = f64(bf(w)).reshape(k // 32, 32, n)
    amax = np.abs(w).max(1)
    if fmt == "e4m3":
        byte = np.frexp(amax)[1] - 1 + 127 - 7
    else:
        mant, ex = np.frexp(amax / 6.0)
        byte = np.where(mant > 0.5, ex, ex - 1) + 127
    byte = np.clip(np.where(amax > 0, byte, 1), 1, 254)
    scaled = (w * np.exp2(127.0 - byte)[:, None, :]).reshape(k, n).astype(np.float32)
    by_word = np.ascontiguousarray(scaled.reshape(k // 512, 128, 4, n).transpose(0, 1, 3, 2))
    if fmt == "e4m3":
        words = by_word.astype(ml_dtypes.float8_e4m3fn).view(np.uint8)
    else:
        c = by_word.astype(ml_dtypes.float4_e2m1fn).view(np.uint8) & 0xF
        words = c[..., 0::2] | (c[..., 1::2] << 4)
    return np.ascontiguousarray(words), np.ascontiguousarray(byte.astype(np.uint8).reshape(k // 512, 16, n))


def unpack_weight(words, scales, fmt):
    g, p, n, _ = words.shape
    if fmt == "e4m3":
        vals = np.ascontiguousarray(words).view(ml_dtypes.float8_e4m3fn).astype(np.float64)
    else:
        nib = np.empty((g, p, n, 4), np.uint8)
        nib[..., 0::2] = words & 0xF
        nib[..., 1::2] = words >> 4
        vals = E2M1[nib]
    vals = vals * np.repeat(np.exp2(scales.astype(np.float64) - 127.0), 8, axis=1)[..., None]
    return vals.transpose(0, 1, 3, 2).reshape(g * 512, n)


M, B, T, D, P = 3, 2048, 4, 512, 128
LN_EPS = 1e-5
NORM_EPS = 1e-12


def erf(v):
    a = np.clip(v, -6.0, 6.0)
    term = a.copy()
    total = a.copy()
    for n in range(1, 130):
        term = term * (2.0 * a * a / (2 * n + 1))
        total = total + term
    return 2.0 / np.sqrt(np.pi) * np.exp(-a * a) * total


def gelu_erf(v):
    return 0.5 * v * (1.0 + erf(v / np.sqrt(2.0)))


def setup_inputs():
    s = mx_kscale(D)
    feats = bf(np.random.standard_normal((M, B, T, D)) * s)
    w1 = np.random.standard_normal((M, D, D)) * np.sqrt(T / D) / s[None, :, None]
    b1 = bf(np.random.standard_normal((M, D)) * 0.3)
    w2 = np.random.standard_normal((M, D, P)) * 0.6 / np.sqrt(D)
    b2 = bf(0.25 + np.random.standard_normal((M, P)) * 0.15)
    gamma = bf(1.0 + np.random.standard_normal((M, P)) * 0.2)
    beta = bf(np.random.standard_normal((M, P)) * 0.3)
    w1_words, w1_scales = pack_weight(w1.reshape(-1, D), "e4m3")
    w2_words, w2_scales = pack_weight(w2.reshape(-1, P), "e4m3")
    return {"feats": feats,
            "W1_words": w1_words,
            "W1_scales": w1_scales,
            "b1": b1,
            "W2_words": w2_words,
            "W2_scales": w2_scales,
            "b2": b2,
            "gamma": gamma,
            "beta": beta}


def reference(feats, W1_words, W1_scales, b1, W2_words, W2_scales, b2, gamma, beta):
    pooled = f64(feats).mean(axis=2)
    h = gelu_erf((mxq(pooled, 2, "e4m3") @ unpack_weight(W1_words, W1_scales, "e4m3").reshape(M, D, D)) + f64(b1)[:, None, :])
    z = (mxq(h, 2, "e4m3") @ unpack_weight(W2_words, W2_scales, "e4m3").reshape(M, D, P)) + f64(b2)[:, None, :]
    mu = z.mean(axis=-1, keepdims=True)
    var = np.mean((z - mu) ** 2, axis=-1, keepdims=True)
    z = (z - mu) / np.sqrt(var + LN_EPS) * f64(gamma)[:, None, :] + f64(beta)[:, None, :]
    n = np.sqrt(np.sum(z * z, axis=-1, keepdims=True))
    return z / np.maximum(n, NORM_EPS)

@@ -1,0 +1,311 @@
+from contextlib import ExitStack
+
+import concourse.mybir as mybir
+from concourse.masks import make_identity
+
+F32 = mybir.dt.float32
+BF16 = mybir.dt.bfloat16
+I32 = mybir.dt.int32
+U32 = mybir.dt.uint32
+U8 = mybir.dt.uint8
+FP8X4 = mybir.dt.float8_e4m3fn_x4
+ALU = mybir.AluOpType
+ACT = mybir.ActivationFunctionType
+
+P = 128
+PACK = 4
+MODS = 3
+BATCH = 2048
+STEPS = 4
+D = 512
+PROJ = 128
+TILES = 4
+GROUP = TILES * P
+GROUPS = BATCH // GROUP
+TOTAL = MODS * GROUPS
+HALF = TILES // 2
+SLICES = D // P
+LN_EPS = 1e-5
+NORM_EPS = 1e-12
+
+FLOPS = 2 * MODS * BATCH * (D * D + D * PROJ)
+
+
+def tile_semanticaligner_t_e_kernel(
+    tc, feats, W1_words, W1_scales, b1, W2_words, W2_scales, b2, gamma, beta, out
+):
+    nc = tc.nc
+    with ExitStack() as ctx:
+        ctx.enter_context(tc.manual_schedule())
+        consts = ctx.enter_context(tc.tile_pool(name="consts", bufs=1))
+        loads = ctx.enter_context(tc.tile_pool(name="loads", bufs=6))
+        work = ctx.enter_context(tc.tile_pool(name="work", bufs=2))
+        psum_t = ctx.enter_context(tc.psum_pool(name="psum_t", bufs=3))
+        psum_z1 = ctx.enter_context(tc.psum_pool(name="psum_z1", bufs=4))
+        psum_z = ctx.enter_context(tc.psum_pool(name="psum_z", bufs=1))
+
+        x_of, pairs_of, pooled_of, pooled_mx, h_turned_of, h_of, h_mx = {}, {}, {}, {}, {}, {}, {}
+        grouped_of, z_of, neg_mean_of, rstd_of, gained_of, y_of, norm_sq_of, inv_norm_of = {}, {}, {}, {}, {}, {}, {}, {}
+
+        def load(n, half):
+            if n >= TOTAL:
+                return
+            m, g = divmod(n, GROUPS)
+            x = loads.tile([P, HALF, STEPS, D], BF16, name="x")
+            rows = feats[m, GROUP * g : GROUP * (g + 1)].rearrange("(p i) t d -> p i t d", i=TILES)
+            nc.sync.dma_start(out=x[:], in_=rows[:, HALF * half : HALF * (half + 1)])
+            x_of[(n, half)] = x
+
+        load(0, 0)
+        load(0, 1)
+
+        ident_f32 = consts.tile([P, P], F32)
+        make_identity(nc, ident_f32[:])
+        ident_bf16 = consts.tile([P, P], BF16)
+        make_identity(nc, ident_bf16[:])
+
+        w1_planes = consts.tile([P, MODS, D], U8, align_bytes=64)
+        w2_planes = consts.tile([P, MODS, PROJ], U8, align_bytes=64)
+        nc.vector.memset(w1_planes[:].bitcast(I32), 0)
+        nc.vector.memset(w2_planes[:].bitcast(I32), 0)
+        b1_rows = consts.tile([P, P], BF16)
+        nc.vector.memset(b1_rows[:], 0.0)
+        minus_half = consts.tile([P, TILES], F32)
+        nc.vector.memset(minus_half[:], -0.5)
+        for quad in range(4):
+            nc.sync.dma_start(
+                out=w1_planes[32 * quad : 32 * quad + 4].bitcast(I32),
+                in_=W1_scales[:, 4 * quad : 4 * quad + 4, :].rearrange("g r n -> r g n").bitcast(I32),
+            )
+        w1_words = consts.tile([P, MODS, PACK * D], U8, align_bytes=64)
+        nc.sync.dma_start(
+            out=w1_words[:].bitcast(I32), in_=W1_words.rearrange("g p n t -> p g (n t)").bitcast(I32)
+        )
+        nc.sync.dma_start(out=b1_rows[0 : MODS * SLICES, :], in_=b1.rearrange("m (j c) -> (m j) c", c=P))
+        load(1, 0)
+        load(1, 1)
+        for quad in range(4):
+            nc.sync.dma_start(
+                out=w2_planes[32 * quad : 32 * quad + 4].bitcast(I32),
+                in_=W2_scales[:, 4 * quad : 4 * quad + 4, :].rearrange("g r n -> r g n").bitcast(I32),
+            )
+        w2_words = consts.tile([P, MODS, PACK * PROJ], U8, align_bytes=64)
+        nc.sync.dma_start(
+            out=w2_words[:].bitcast(I32), in_=W2_words.rearrange("g p n t -> p g (n t)").bitcast(I32)
+        )
+        b2_all = consts.tile([P, MODS, PROJ], BF16)
+        gamma_all = consts.tile([P, MODS, PROJ], BF16)
+        beta_all = consts.tile([P, MODS, PROJ], BF16)
+        for row_tile, vec in ((b2_all, b2), (gamma_all, gamma), (beta_all, beta)):
+            nc.sync.dma_start(
+                out=row_tile[:].rearrange("p m c -> p (m c)"),
+                in_=vec.rearrange("m c -> (m c)").partition_broadcast(P),
+            )
+        load(2, 0)
+        load(2, 1)
+
+        b1_turned = psum_t.tile([P, P], BF16, tag="t")
+        nc.tensor.transpose(b1_turned[:], b1_rows[:], ident_bf16[:])
+        b1_cols = consts.tile([P, MODS * SLICES], F32)
+        nc.scalar.copy(out=b1_cols[:], in_=b1_turned[:, 0 : MODS * SLICES])
+
+        def add_pairs(n, half):
+            pairs = work.tile([P, HALF * 2, D], F32, name="pairs")
+            x_pairs = x_of[(n, half)][:].rearrange("p i (h e) d -> p (i h) e d", e=2)
+            nc.vector.tensor_tensor(out=pairs[:], in0=x_pairs[:, :, 0, :], in1=x_pairs[:, :, 1, :], op=ALU.add)
+            pairs_of[(n, half)] = pairs
+            load(n + 3, half)
+
+        def add_halves(n, half):
+            if half == 0:
+                pooled = work.tile([P, TILES, D], BF16, name="pooled")
+                pooled_of[n] = pooled
+            halves = pairs_of[(n, half)][:].rearrange("p (i h) d -> p i h d", h=2)
+            nc.vector.tensor_tensor(
+                out=pooled_of[n][:, HALF * half : HALF * (half + 1), :],
+                in0=halves[:, :, 0, :], in1=halves[:, :, 1, :], op=ALU.add,
+            )
+
+        def turn_rows(src, key):
+            src_words = src[:].bitcast(F32)
+            grouped = work.tile([P, GROUP, PACK], BF16, name="grouped", align_bytes=64)
+            grouped_words = grouped[:].bitcast(F32)
+            for half in range(2):
+                turned = psum_t.tile([P, 2, HALF * P], F32, name="turned", tag="t")
+                for i in range(HALF):
+                    for u in range(2):
+                        nc.tensor.transpose(
+                            turned[:, u, P * i : P * (i + 1)],
+                            src_words[:, HALF * half + i, u : D // 2 : 2],
+                            ident_f32[:],
+                        )
+                nc.scalar.copy(
+                    out=grouped_words[:, HALF * P * half : HALF * P * (half + 1), :],
+                    in_=turned[:].rearrange("p u c -> p c u"),
+                )
+            grouped_of[key] = grouped
+
+        def quantise(key):
+            codes = work.tile([P, GROUP], U32, name="codes", align_bytes=64)
+            planes = work.tile([P, GROUP], U8, name="planes", align_bytes=64)
+            nc.vector.quantize_mx(
+                out=codes[:].bitcast(FP8X4), scales=planes[:],
+                in_=grouped_of[key][:].rearrange("p c t -> p (c t)"),
+            )
+            return codes, planes
+
+        def turn_pooled(n):
+            turn_rows(pooled_of[n], ("pooled", n))
+
+        def quantise_pooled(n):
+            pooled_mx[n] = quantise(("pooled", n))
+
+        def hidden(n):
+            m = n // GROUPS
+            codes, planes = pooled_mx[n]
+            h_turned = work.tile([P, SLICES, GROUP], BF16, name="h_turned")
+            for j in range(SLICES):
+                z1 = psum_z1.tile([P, GROUP], F32, name="z1")
+                nc.tensor.matmul_mx(
+                    out=z1[:],
+                    lhsT=w1_words[:, m, PACK * P * j : PACK * P * (j + 1)].bitcast(FP8X4),
+                    lhsT_scale=w1_planes[:, m, P * j : P * (j + 1)],
+                    rhs=codes[:].bitcast(FP8X4),
+                    rhs_scale=planes[:],
+                    start=True,
+                    stop=True,
+                )
+                nc.scalar.activation(
+                    out=h_turned[:, j, :], in_=z1[:], func=ACT.Gelu,
+                    bias=b1_cols[:, SLICES * m + j : SLICES * m + j + 1], scale=1.0 / STEPS,
+                )
+            h_turned_of[n] = h_turned
+
+        def turn_back(n):
+            h_turned = h_turned_of[n]
+            h = work.tile([P, TILES, D], BF16, name="h")
+            for half in range(2):
+                h_rows = psum_t.tile([P, HALF, D], BF16, name="h_rows", tag="t")
+                for i in range(HALF):
+                    col = P * (HALF * half + i)
+                    for j in range(SLICES):
+                        nc.tensor.transpose(
+                            h_rows[:, i, P * j : P * (j + 1)], h_turned[:, j, col : col + P], ident_bf16[:]
+                        )
+                nc.scalar.copy(out=h[:, HALF * half : HALF * (half + 1), :], in_=h_rows[:])
+            h_of[n] = h
+
+        def turn_h(n):
+            turn_rows(h_of[n], ("h", n))
+
+        def quantise_h(n):
+            h_mx[n] = quantise(("h", n))
+
+        def project(n):
+            m = n // GROUPS
+            codes, planes = h_mx[n]
+            z_acc = psum_z.tile([P, TILES, PROJ], F32, name="z_acc")
+            for i in range(TILES):
+                nc.tensor.matmul_mx(
+                    out=z_acc[:, i, :],
+                    lhsT=codes[:, P * i : P * (i + 1)].bitcast(FP8X4),
+                    lhsT_scale=planes[:, P * i : P * (i + 1)],
+                    rhs=w2_words[:, m, :].bitcast(FP8X4),
+                    rhs_scale=w2_planes[:, m, :],
+                    start=True,
+                    stop=True,
+                )
+            z = work.tile([P, TILES, PROJ], F32, name="z")
+            z_sum = work.tile([P, TILES], F32, name="z_sum")
+            for i in range(TILES):
+                nc.vector.scalar_tensor_tensor(
+                    out=z[:, i, :], in0=z_acc[:, i, :], scalar=1.0, in1=b2_all[:, m, :],
+                    op0=ALU.mult, op1=ALU.add, accum_out=z_sum[:, i : i + 1],
+                )
+            neg_mean = work.tile([P, TILES], F32, name="neg_mean")
+            nc.vector.tensor_scalar_mul(out=neg_mean[:], in0=z_sum[:], scalar1=-1.0 / PROJ)
+            z_of[n] = z
+            neg_mean_of[n] = neg_mean
+
+        def apply_gain(n):
+            m = n // GROUPS
+            gained = work.tile([P, TILES, PROJ], F32, name="gained")
+            for i in range(TILES):
+                nc.vector.scalar_tensor_tensor(
+                    out=gained[:, i, :], in0=z_of[n][:, i, :], scalar=neg_mean_of[n][:, i : i + 1],
+                    in1=gamma_all[:, m, :], op0=ALU.add, op1=ALU.mult,
+                )
+            gained_of[n] = gained
+
+        def variance(n):
+            squares = work.tile([P, TILES, PROJ], F32, name="squares")
+            dev_sum = work.tile([P, TILES], F32, name="dev_sum")
+            for i in range(TILES):
+                nc.scalar.activation(
+                    out=squares[:, i, :], in_=z_of[n][:, i, :], func=ACT.Square,
+                    bias=neg_mean_of[n][:, i : i + 1], scale=1.0, accum_out=dev_sum[:, i : i + 1],
+                )
+            var_eps = work.tile([P, TILES], F32, name="var_eps")
+            nc.vector.tensor_scalar(
+                out=var_eps[:], in0=dev_sum[:], scalar1=1.0 / PROJ, scalar2=LN_EPS, op0=ALU.mult, op1=ALU.add
+            )
+            rstd = work.tile([P, TILES], F32, name="rstd")
+            nc.gpsimd.tensor_tensor(out=rstd[:], in0=var_eps[:], in1=minus_half[:], op=ALU.pow)
+            rstd_of[n] = rstd
+
+        def shift_and_square(n):
+            m = n // GROUPS
+            y = work.tile([P, TILES, PROJ], F32, name="y")
+            for i in range(TILES):
+                nc.vector.scalar_tensor_tensor(
+                    out=y[:, i, :], in0=gained_of[n][:, i, :], scalar=rstd_of[n][:, i : i + 1],
+                    in1=beta_all[:, m, :], op0=ALU.mult, op1=ALU.add,
+                )
+            y_squares = work.tile([P, TILES, PROJ], F32, name="y_squares")
+            norm_sq = work.tile([P, TILES], F32, name="norm_sq")
+            for i in range(TILES):
+                nc.scalar.activation(
+                    out=y_squares[:, i, :], in_=y[:, i, :], func=ACT.Square, accum_out=norm_sq[:, i : i + 1]
+                )
+            y_of[n] = y
+            norm_sq_of[n] = norm_sq
+
+        def inverse_norm(n):
+            norm_floor = work.tile([P, TILES], F32, name="norm_floor")
+            nc.vector.tensor_scalar_max(out=norm_floor[:], in0=norm_sq_of[n][:], scalar1=NORM_EPS * NORM_EPS)
+            inv_norm = work.tile([P, TILES], F32, name="inv_norm")
+            nc.gpsimd.tensor_tensor(out=inv_norm[:], in0=norm_floor[:], in1=minus_half[:], op=ALU.pow)
+            inv_norm_of[n] = inv_norm
+
+        def finish(n):
+            m, g = divmod(n, GROUPS)
+            result = work.tile([P, TILES, PROJ], F32, name="result")
+            for i in range(TILES):
+                nc.scalar.activation(
+                    out=result[:, i, :], in_=y_of[n][:, i, :], func=ACT.Copy, scale=inv_norm_of[n][:, i : i + 1]
+                )
+            nc.scalar.dma_start(
+                out=out[m, GROUP * g : GROUP * (g + 1), :].rearrange("(p i) c -> p i c", i=TILES), in_=result[:]
+            )
+
+        def run(stage, n, *args):
+            if 0 <= n < TOTAL:
+                stage(n, *args)
+
+        for n in range(-2, TOTAL + 2):
+            run(hidden, n)
+            run(finish, n - 2)
+            run(add_pairs, n + 2, 0)
+            run(apply_gain, n - 1)
+            run(add_halves, n + 2, 0)
+            run(variance, n - 1)
+            run(turn_back, n)
+            run(add_pairs, n + 2, 1)
+            run(turn_pooled, n + 1)
+            run(turn_h, n)
+            run(shift_and_square, n - 1)
+            run(add_halves, n + 2, 1)
+            run(quantise_h, n)
+            run(quantise_pooled, n + 1)
+            run(inverse_norm, n - 1)
+            run(project, n)

@@ -23,7 +23,10 @@ TILES = 4
 GROUP = TILES * P
 GROUPS = BATCH // GROUP
 TOTAL = MODS * GROUPS
-HALF = TILES // 2
+VTILES = 3
+VROWS = VTILES * P
+CHUNK = P // STEPS
+HALF_D = D // 2
 SLICES = D // P
 LN_EPS = 1e-5
 NORM_EPS = 1e-12
@@ -38,26 +41,28 @@ def tile_semanticaligner_t_e_kernel(
     with ExitStack() as ctx:
         ctx.enter_context(tc.manual_schedule())
         consts = ctx.enter_context(tc.tile_pool(name="consts", bufs=1))
-        loads = ctx.enter_context(tc.tile_pool(name="loads", bufs=6))
+        loads = ctx.enter_context(tc.tile_pool(name="loads", bufs=4))
         work = ctx.enter_context(tc.tile_pool(name="work", bufs=2))
         psum_t = ctx.enter_context(tc.psum_pool(name="psum_t", bufs=3))
         psum_z1 = ctx.enter_context(tc.psum_pool(name="psum_z1", bufs=4))
         psum_z = ctx.enter_context(tc.psum_pool(name="psum_z", bufs=1))
 
-        x_of, pairs_of, pooled_of, pooled_mx, h_turned_of, h_of, h_mx = {}, {}, {}, {}, {}, {}, {}
+        x_of, steps_of, sums_of, pairs_of, pooled_of, pooled_mx, h_turned_of, h_of, h_mx = {}, {}, {}, {}, {}, {}, {}, {}, {}
         grouped_of, z_of, neg_mean_of, rstd_of, gained_of, y_of, norm_sq_of, inv_norm_of = {}, {}, {}, {}, {}, {}, {}, {}
 
-        def load(n, half):
+        def load(n):
             if n >= TOTAL:
                 return
             m, g = divmod(n, GROUPS)
-            x = loads.tile([P, HALF, STEPS, D], BF16, name="x")
-            rows = feats[m, GROUP * g : GROUP * (g + 1)].rearrange("(p i) t d -> p i t d", i=TILES)
-            nc.sync.dma_start(out=x[:], in_=rows[:, HALF * half : HALF * (half + 1)])
-            x_of[(n, half)] = x
+            rows = feats[m, GROUP * g : GROUP * (g + 1)]
+            x = loads.tile([P, VTILES, STEPS, D], BF16, name="x")
+            nc.sync.dma_start(out=x[:], in_=rows[0:VROWS].rearrange("(p i) t d -> p i t d", i=VTILES))
+            x_of[n] = x
+            steps = loads.tile([P, P // CHUNK, D], BF16, name="steps")
+            nc.sync.dma_start(out=steps[:], in_=rows[VROWS:GROUP].rearrange("(c l) t d -> (l t) c d", l=CHUNK))
+            steps_of[n] = steps
 
-        load(0, 0)
-        load(0, 1)
+        load(0)
 
         ident_f32 = consts.tile([P, P], F32)
         make_identity(nc, ident_f32[:])
@@ -82,8 +87,7 @@ def tile_semanticaligner_t_e_kernel(
             out=w1_words[:].bitcast(I32), in_=W1_words.rearrange("g p n t -> p g (n t)").bitcast(I32)
         )
         nc.sync.dma_start(out=b1_rows[0 : MODS * SLICES, :], in_=b1.rearrange("m (j c) -> (m j) c", c=P))
-        load(1, 0)
-        load(1, 1)
+        load(1)
         for quad in range(4):
             nc.sync.dma_start(
                 out=w2_planes[32 * quad : 32 * quad + 4].bitcast(I32),
@@ -101,8 +105,15 @@ def tile_semanticaligner_t_e_kernel(
                 out=row_tile[:].rearrange("p m c -> p (m c)"),
                 in_=vec.rearrange("m c -> (m c)").partition_broadcast(P),
             )
-        load(2, 0)
-        load(2, 1)
+        load(2)
+
+        same_row_f32 = consts.tile([P, CHUNK], F32)
+        nc.vector.tensor_reduce(
+            out=same_row_f32[:], in_=ident_f32[:].rearrange("p (l t) -> p l t", t=STEPS),
+            axis=mybir.AxisListType.X, op=ALU.add,
+        )
+        same_row = consts.tile([P, CHUNK], BF16)
+        nc.vector.tensor_copy(out=same_row[:], in_=same_row_f32[:])
 
         b1_turned = psum_t.tile([P, P], BF16, tag="t")
         nc.tensor.transpose(b1_turned[:], b1_rows[:], ident_bf16[:])
@@ -110,40 +121,59 @@ def tile_semanticaligner_t_e_kernel(
         nc.scalar.copy(out=b1_cols[:], in_=b1_turned[:, 0 : MODS * SLICES])
 
         def add_pairs(n, half):
-            pairs = work.tile([P, HALF * 2, D], F32, name="pairs")
-            x_pairs = x_of[(n, half)][:].rearrange("p i (h e) d -> p (i h) e d", e=2)
-            nc.vector.tensor_tensor(out=pairs[:], in0=x_pairs[:, :, 0, :], in1=x_pairs[:, :, 1, :], op=ALU.add)
+            cols = slice(HALF_D * half, HALF_D * (half + 1))
+            pairs = work.tile([P, VTILES * 2, HALF_D], F32, name="pairs")
+            x_pairs = x_of[n][:].rearrange("p i (h e) d -> p (i h) e d", e=2)
+            nc.vector.tensor_tensor(
+                out=pairs[:], in0=x_pairs[:, :, 0, cols], in1=x_pairs[:, :, 1, cols], op=ALU.add
+            )
             pairs_of[(n, half)] = pairs
-            load(n + 3, half)
 
         def add_halves(n, half):
+            cols = slice(HALF_D * half, HALF_D * (half + 1))
             if half == 0:
-                pooled = work.tile([P, TILES, D], BF16, name="pooled")
+                pooled = work.tile([P, VTILES, D], BF16, name="pooled")
                 pooled_of[n] = pooled
             halves = pairs_of[(n, half)][:].rearrange("p (i h) d -> p i h d", h=2)
             nc.vector.tensor_tensor(
-                out=pooled_of[n][:, HALF * half : HALF * (half + 1), :],
-                in0=halves[:, :, 0, :], in1=halves[:, :, 1, :], op=ALU.add,
+                out=pooled_of[n][:, :, cols], in0=halves[:, :, 0, :], in1=halves[:, :, 1, :], op=ALU.add
             )
 
-        def turn_rows(src, key):
-            src_words = src[:].bitcast(F32)
+        def add_steps(n):
+            steps = steps_of[n]
+            sums = psum_t.tile([P, PACK, P], F32, name="sums", tag="t")
+            for c in range(P // CHUNK):
+                for t in range(PACK):
+                    nc.tensor.matmul(
+                        out=sums[:, t, CHUNK * c : CHUNK * (c + 1)],
+                        lhsT=steps[:, c, t:D:PACK],
+                        rhs=same_row[:],
+                        start=True,
+                        stop=True,
+                    )
+            sums_of[n] = sums
+            load(n + 3)
+
+        def round_steps(n):
             grouped = work.tile([P, GROUP, PACK], BF16, name="grouped", align_bytes=64)
+            nc.vector.tensor_copy(out=grouped[:, VROWS:GROUP, :], in_=sums_of[n][:].rearrange("p t c -> p c t"))
+            grouped_of[("pooled", n)] = grouped
+
+        def turn_rows(src, tiles, grouped):
+            src_words = src[:].bitcast(F32)
             grouped_words = grouped[:].bitcast(F32)
-            for half in range(2):
-                turned = psum_t.tile([P, 2, HALF * P], F32, name="turned", tag="t")
-                for i in range(HALF):
+            for first in range(0, tiles, 2):
+                count = min(2, tiles - first)
+                turned = psum_t.tile([P, 2, count * P], F32, name="turned", tag="t")
+                for i in range(count):
                     for u in range(2):
                         nc.tensor.transpose(
-                            turned[:, u, P * i : P * (i + 1)],
-                            src_words[:, HALF * half + i, u : D // 2 : 2],
-                            ident_f32[:],
+                            turned[:, u, P * i : P * (i + 1)], src_words[:, first + i, u : D // 2 : 2], ident_f32[:]
                         )
                 nc.scalar.copy(
-                    out=grouped_words[:, HALF * P * half : HALF * P * (half + 1), :],
+                    out=grouped_words[:, P * first : P * (first + count), :],
                     in_=turned[:].rearrange("p u c -> p c u"),
                 )
-            grouped_of[key] = grouped
 
         def quantise(key):
             codes = work.tile([P, GROUP], U32, name="codes", align_bytes=64)
@@ -155,7 +185,7 @@ def tile_semanticaligner_t_e_kernel(
             return codes, planes
 
         def turn_pooled(n):
-            turn_rows(pooled_of[n], ("pooled", n))
+            turn_rows(pooled_of[n], VTILES, grouped_of[("pooled", n)])
 
         def quantise_pooled(n):
             pooled_mx[n] = quantise(("pooled", n))
@@ -184,19 +214,21 @@ def tile_semanticaligner_t_e_kernel(
         def turn_back(n):
             h_turned = h_turned_of[n]
             h = work.tile([P, TILES, D], BF16, name="h")
-            for half in range(2):
-                h_rows = psum_t.tile([P, HALF, D], BF16, name="h_rows", tag="t")
-                for i in range(HALF):
-                    col = P * (HALF * half + i)
+            for first in range(0, TILES, 2):
+                h_rows = psum_t.tile([P, 2, D], BF16, name="h_rows", tag="t")
+                for i in range(2):
+                    col = P * (first + i)
                     for j in range(SLICES):
                         nc.tensor.transpose(
                             h_rows[:, i, P * j : P * (j + 1)], h_turned[:, j, col : col + P], ident_bf16[:]
                         )
-                nc.scalar.copy(out=h[:, HALF * half : HALF * (half + 1), :], in_=h_rows[:])
+                nc.scalar.copy(out=h[:, first : first + 2, :], in_=h_rows[:])
             h_of[n] = h
 
         def turn_h(n):
-            turn_rows(h_of[n], ("h", n))
+            grouped = work.tile([P, GROUP, PACK], BF16, name="grouped", align_bytes=64)
+            turn_rows(h_of[n], TILES, grouped)
+            grouped_of[("h", n)] = grouped
 
         def quantise_h(n):
             h_mx[n] = quantise(("h", n))
@@ -284,9 +316,11 @@ def tile_semanticaligner_t_e_kernel(
                 nc.scalar.activation(
                     out=result[:, i, :], in_=y_of[n][:, i, :], func=ACT.Copy, scale=inv_norm_of[n][:, i : i + 1]
                 )
+            rows = out[m, GROUP * g : GROUP * (g + 1), :]
             nc.scalar.dma_start(
-                out=out[m, GROUP * g : GROUP * (g + 1), :].rearrange("(p i) c -> p i c", i=TILES), in_=result[:]
+                out=rows[0:VROWS].rearrange("(p i) c -> p i c", i=VTILES), in_=result[:, 0:VTILES, :]
             )
+            nc.scalar.dma_start(out=rows[VROWS:GROUP], in_=result[:, VTILES, :])
 
         def run(stage, n, *args):
             if 0 <= n < TOTAL:
@@ -294,10 +328,12 @@ def tile_semanticaligner_t_e_kernel(
 
         for n in range(-2, TOTAL + 2):
             run(hidden, n)
+            run(add_steps, n + 1)
             run(finish, n - 2)
             run(add_pairs, n + 2, 0)
             run(apply_gain, n - 1)
             run(add_halves, n + 2, 0)
+            run(round_steps, n + 1)
             run(variance, n - 1)
             run(turn_back, n)
             run(add_pairs, n + 2, 1)

@@ -327,12 +327,13 @@ def tile_semanticaligner_t_e_kernel(
                 stage(n, *args)
 
         for n in range(-2, TOTAL + 2):
+            run(inverse_norm, n - 2)
             run(hidden, n)
+            run(add_pairs, n + 2, 0)
+            run(project, n - 1)
             run(add_steps, n + 1)
             run(finish, n - 2)
-            run(add_pairs, n + 2, 0)
             run(apply_gain, n - 1)
-            run(add_halves, n + 2, 0)
             run(round_steps, n + 1)
             run(variance, n - 1)
             run(turn_back, n)
@@ -340,8 +341,7 @@ def tile_semanticaligner_t_e_kernel(
             run(turn_pooled, n + 1)
             run(turn_h, n)
             run(shift_and_square, n - 1)
+            run(quantise_pooled, n + 1)
+            run(add_halves, n + 2, 0)
             run(add_halves, n + 2, 1)
             run(quantise_h, n)
-            run(quantise_pooled, n + 1)
-            run(inverse_norm, n - 1)
-            run(project, n)

@@ -48,6 +48,7 @@ def tile_semanticaligner_t_e_kernel(
         psum_z = ctx.enter_context(tc.psum_pool(name="psum_z", bufs=1))
 
         x_of, steps_of, sums_of, pairs_of, pooled_of, pooled_mx, h_turned_of, h_of, h_mx = {}, {}, {}, {}, {}, {}, {}, {}, {}
+        z_acc_of, dev_sum_of = {}, {}
         grouped_of, z_of, neg_mean_of, rstd_of, gained_of, y_of, norm_sq_of, inv_norm_of = {}, {}, {}, {}, {}, {}, {}, {}
 
         def load(n):
@@ -247,6 +248,11 @@ def tile_semanticaligner_t_e_kernel(
                     start=True,
                     stop=True,
                 )
+            z_acc_of[n] = z_acc
+
+        def bias_and_mean(n):
+            m = n // GROUPS
+            z_acc = z_acc_of[n]
             z = work.tile([P, TILES, PROJ], F32, name="z")
             z_sum = work.tile([P, TILES], F32, name="z_sum")
             for i in range(TILES):
@@ -269,7 +275,7 @@ def tile_semanticaligner_t_e_kernel(
                 )
             gained_of[n] = gained
 
-        def variance(n):
+        def square_deviations(n):
             squares = work.tile([P, TILES, PROJ], F32, name="squares")
             dev_sum = work.tile([P, TILES], F32, name="dev_sum")
             for i in range(TILES):
@@ -277,9 +283,12 @@ def tile_semanticaligner_t_e_kernel(
                     out=squares[:, i, :], in_=z_of[n][:, i, :], func=ACT.Square,
                     bias=neg_mean_of[n][:, i : i + 1], scale=1.0, accum_out=dev_sum[:, i : i + 1],
                 )
+            dev_sum_of[n] = dev_sum
+
+        def inverse_std(n):
             var_eps = work.tile([P, TILES], F32, name="var_eps")
             nc.vector.tensor_scalar(
-                out=var_eps[:], in0=dev_sum[:], scalar1=1.0 / PROJ, scalar2=LN_EPS, op0=ALU.mult, op1=ALU.add
+                out=var_eps[:], in0=dev_sum_of[n][:], scalar1=1.0 / PROJ, scalar2=LN_EPS, op0=ALU.mult, op1=ALU.add
             )
             rstd = work.tile([P, TILES], F32, name="rstd")
             nc.gpsimd.tensor_tensor(out=rstd[:], in0=var_eps[:], in1=minus_half[:], op=ALU.pow)
@@ -328,20 +337,22 @@ def tile_semanticaligner_t_e_kernel(
 
         for n in range(-2, TOTAL + 2):
             run(inverse_norm, n - 2)
-            run(hidden, n)
-            run(add_pairs, n + 2, 0)
-            run(project, n - 1)
-            run(add_steps, n + 1)
-            run(finish, n - 2)
+            run(bias_and_mean, n - 1)
             run(apply_gain, n - 1)
+            run(square_deviations, n - 1)
+            run(add_pairs, n + 2, 0)
+            run(inverse_std, n - 1)
             run(round_steps, n + 1)
-            run(variance, n - 1)
+            run(finish, n - 2)
             run(turn_back, n)
             run(add_pairs, n + 2, 1)
             run(turn_pooled, n + 1)
             run(turn_h, n)
             run(shift_and_square, n - 1)
             run(quantise_pooled, n + 1)
+            run(quantise_h, n)
+            run(hidden, n + 1)
+            run(project, n)
+            run(add_steps, n + 2)
             run(add_halves, n + 2, 0)
             run(add_halves, n + 2, 1)
-            run(quantise_h, n)

@@ -343,16 +343,16 @@ def tile_semanticaligner_t_e_kernel(
             run(add_pairs, n + 2, 0)
             run(inverse_std, n - 1)
             run(round_steps, n + 1)
-            run(finish, n - 2)
             run(turn_back, n)
+            run(finish, n - 2)
             run(add_pairs, n + 2, 1)
             run(turn_pooled, n + 1)
             run(turn_h, n)
             run(shift_and_square, n - 1)
             run(quantise_pooled, n + 1)
+            run(add_halves, n + 2, 0)
             run(quantise_h, n)
             run(hidden, n + 1)
             run(project, n)
             run(add_steps, n + 2)
-            run(add_halves, n + 2, 0)
             run(add_halves, n + 2, 1)

@@ -23,11 +23,10 @@ TILES = 4
 GROUP = TILES * P
 GROUPS = BATCH // GROUP
 TOTAL = MODS * GROUPS
-VTILES = 3
+VTILES = 2
 VROWS = VTILES * P
 CHUNK = P // STEPS
-HALF_D = D // 2
-SLICES = D // P
+CHUNKS = (GROUP - VROWS) // CHUNK
 LN_EPS = 1e-5
 NORM_EPS = 1e-12
 
@@ -42,13 +41,15 @@ def tile_semanticaligner_t_e_kernel(
         ctx.enter_context(tc.manual_schedule())
         consts = ctx.enter_context(tc.tile_pool(name="consts", bufs=1))
         loads = ctx.enter_context(tc.tile_pool(name="loads", bufs=4))
-        work = ctx.enter_context(tc.tile_pool(name="work", bufs=2))
+        work = ctx.enter_context(tc.tile_pool(name="work", bufs=3))
         psum_t = ctx.enter_context(tc.psum_pool(name="psum_t", bufs=3))
         psum_z1 = ctx.enter_context(tc.psum_pool(name="psum_z1", bufs=4))
         psum_z = ctx.enter_context(tc.psum_pool(name="psum_z", bufs=1))
 
-        x_of, steps_of, sums_of, pairs_of, pooled_of, pooled_mx, h_turned_of, h_of, h_mx = {}, {}, {}, {}, {}, {}, {}, {}, {}
-        z_acc_of, dev_sum_of = {}, {}
+        x_of, steps_of, sums_of, pairs_of, pooled_of, turned_of, pooled_mx, z1_of, h_turned_of, h_mx = (
+            {}, {}, {}, {}, {}, {}, {}, {}, {}, {}
+        )
+        z_acc_of, dev_sum_of, z_sum_of = {}, {}, {}
         grouped_of, z_of, neg_mean_of, rstd_of, gained_of, y_of, norm_sq_of, inv_norm_of = {}, {}, {}, {}, {}, {}, {}, {}
 
         def load(n):
@@ -59,35 +60,29 @@ def tile_semanticaligner_t_e_kernel(
             x = loads.tile([P, VTILES, STEPS, D], BF16, name="x")
             nc.sync.dma_start(out=x[:], in_=rows[0:VROWS].rearrange("(p i) t d -> p i t d", i=VTILES))
             x_of[n] = x
-            steps = loads.tile([P, P // CHUNK, D], BF16, name="steps")
+            steps = loads.tile([P, CHUNKS, D], BF16, name="steps")
             nc.sync.dma_start(out=steps[:], in_=rows[VROWS:GROUP].rearrange("(c l) t d -> (l t) c d", l=CHUNK))
             steps_of[n] = steps
 
-        load(0)
-
-        ident_f32 = consts.tile([P, P], F32)
-        make_identity(nc, ident_f32[:])
-        ident_bf16 = consts.tile([P, P], BF16)
-        make_identity(nc, ident_bf16[:])
-
-        w1_planes = consts.tile([P, MODS, D], U8, align_bytes=64)
+        w1_planes_raw = consts.tile([P, MODS, D], U8, align_bytes=64)
         w2_planes = consts.tile([P, MODS, PROJ], U8, align_bytes=64)
-        nc.vector.memset(w1_planes[:].bitcast(I32), 0)
+        nc.vector.memset(w1_planes_raw[:].bitcast(I32), 0)
         nc.vector.memset(w2_planes[:].bitcast(I32), 0)
-        b1_rows = consts.tile([P, P], BF16)
-        nc.vector.memset(b1_rows[:], 0.0)
         minus_half = consts.tile([P, TILES], F32)
         nc.vector.memset(minus_half[:], -0.5)
+        warm = consts.tile([P, 1], F32)
+        nc.scalar.activation(out=warm[:], in_=minus_half[:, 0:1], func=ACT.Gelu)
+
         for quad in range(4):
             nc.sync.dma_start(
-                out=w1_planes[32 * quad : 32 * quad + 4].bitcast(I32),
+                out=w1_planes_raw[32 * quad : 32 * quad + 4].bitcast(I32),
                 in_=W1_scales[:, 4 * quad : 4 * quad + 4, :].rearrange("g r n -> r g n").bitcast(I32),
             )
-        w1_words = consts.tile([P, MODS, PACK * D], U8, align_bytes=64)
-        nc.sync.dma_start(
-            out=w1_words[:].bitcast(I32), in_=W1_words.rearrange("g p n t -> p g (n t)").bitcast(I32)
-        )
-        nc.sync.dma_start(out=b1_rows[0 : MODS * SLICES, :], in_=b1.rearrange("m (j c) -> (m j) c", c=P))
+        w1_words_raw = consts.tile([P, MODS, D], I32)
+        nc.sync.dma_start(out=w1_words_raw[:], in_=W1_words.rearrange("g p n t -> p g (n t)").bitcast(I32))
+        load(0)
+        b1_raw = consts.tile([P, MODS, PACK], BF16)
+        nc.sync.dma_start(out=b1_raw[:], in_=b1.rearrange("m (p t) -> p m t", t=PACK))
         load(1)
         for quad in range(4):
             nc.sync.dma_start(
@@ -107,7 +102,10 @@ def tile_semanticaligner_t_e_kernel(
                 in_=vec.rearrange("m c -> (m c)").partition_broadcast(P),
             )
         load(2)
+        load(3)
 
+        ident_f32 = consts.tile([P, P], F32)
+        make_identity(nc, ident_f32[:])
         same_row_f32 = consts.tile([P, CHUNK], F32)
         nc.vector.tensor_reduce(
             out=same_row_f32[:], in_=ident_f32[:].rearrange("p (l t) -> p l t", t=STEPS),
@@ -116,64 +114,59 @@ def tile_semanticaligner_t_e_kernel(
         same_row = consts.tile([P, CHUNK], BF16)
         nc.vector.tensor_copy(out=same_row[:], in_=same_row_f32[:])
 
-        b1_turned = psum_t.tile([P, P], BF16, tag="t")
-        nc.tensor.transpose(b1_turned[:], b1_rows[:], ident_bf16[:])
-        b1_cols = consts.tile([P, MODS * SLICES], F32)
-        nc.scalar.copy(out=b1_cols[:], in_=b1_turned[:, 0 : MODS * SLICES])
-
-        def add_pairs(n, half):
-            cols = slice(HALF_D * half, HALF_D * (half + 1))
-            pairs = work.tile([P, VTILES * 2, HALF_D], F32, name="pairs")
-            x_pairs = x_of[n][:].rearrange("p i (h e) d -> p (i h) e d", e=2)
-            nc.vector.tensor_tensor(
-                out=pairs[:], in0=x_pairs[:, :, 0, cols], in1=x_pairs[:, :, 1, cols], op=ALU.add
+        w1_words = consts.tile([P, MODS, PACK, P], I32, align_bytes=64)
+        w1_planes = consts.tile([P, MODS, PACK, P], U8, align_bytes=64)
+        for m in range(MODS):
+            nc.vector.tensor_copy(
+                out=w1_words[:, m, :, :], in_=w1_words_raw[:, m, :].rearrange("p (j t) -> p t j", t=PACK)
             )
-            pairs_of[(n, half)] = pairs
-
-        def add_halves(n, half):
-            cols = slice(HALF_D * half, HALF_D * (half + 1))
-            if half == 0:
-                pooled = work.tile([P, VTILES, D], BF16, name="pooled")
-                pooled_of[n] = pooled
-            halves = pairs_of[(n, half)][:].rearrange("p (i h) d -> p i h d", h=2)
-            nc.vector.tensor_tensor(
-                out=pooled_of[n][:, :, cols], in0=halves[:, :, 0, :], in1=halves[:, :, 1, :], op=ALU.add
+            nc.vector.tensor_copy(
+                out=w1_planes[:, m, :, :].rearrange("p t j -> p j t"),
+                in_=w1_planes_raw[:, m, :].rearrange("p (j t) -> p j t", t=PACK),
             )
+        b1_cols = consts.tile([P, MODS * PACK], F32)
+        nc.vector.tensor_copy(out=b1_cols[:], in_=b1_raw[:].rearrange("p m t -> p (m t)"))
+
+        def add_pairs(n, i):
+            pairs = work.tile([P, 2, D], F32, name="pairs", bufs=4)
+            x_pairs = x_of[n][:].rearrange("p i (h e) d -> p i h e d", e=2)
+            nc.vector.tensor_tensor(out=pairs[:], in0=x_pairs[:, i, :, 0, :], in1=x_pairs[:, i, :, 1, :], op=ALU.add)
+            pairs_of[(n, i)] = pairs
+
+        def turn_pairs(n):
+            for i in range(VTILES):
+                sums = psum_t.tile([P, PACK, P], F32, name="sums", tag="t")
+                for t in range(PACK):
+                    for h in range(2):
+                        nc.tensor.matmul(
+                            out=sums[:, t, :], lhsT=pairs_of[(n, i)][:, h, t:D:PACK], rhs=ident_f32[:],
+                            is_transpose=True, start=(h == 0), stop=(h == 1),
+                        )
+                sums_of[(n, i)] = sums
 
         def add_steps(n):
             steps = steps_of[n]
-            sums = psum_t.tile([P, PACK, P], F32, name="sums", tag="t")
-            for c in range(P // CHUNK):
-                for t in range(PACK):
-                    nc.tensor.matmul(
-                        out=sums[:, t, CHUNK * c : CHUNK * (c + 1)],
-                        lhsT=steps[:, c, t:D:PACK],
-                        rhs=same_row[:],
-                        start=True,
-                        stop=True,
-                    )
-            sums_of[n] = sums
-            load(n + 3)
-
-        def round_steps(n):
-            grouped = work.tile([P, GROUP, PACK], BF16, name="grouped", align_bytes=64)
-            nc.vector.tensor_copy(out=grouped[:, VROWS:GROUP, :], in_=sums_of[n][:].rearrange("p t c -> p c t"))
-            grouped_of[("pooled", n)] = grouped
-
-        def turn_rows(src, tiles, grouped):
-            src_words = src[:].bitcast(F32)
-            grouped_words = grouped[:].bitcast(F32)
-            for first in range(0, tiles, 2):
-                count = min(2, tiles - first)
-                turned = psum_t.tile([P, 2, count * P], F32, name="turned", tag="t")
-                for i in range(count):
-                    for u in range(2):
-                        nc.tensor.transpose(
-                            turned[:, u, P * i : P * (i + 1)], src_words[:, first + i, u : D // 2 : 2], ident_f32[:]
+            for i in range(TILES - VTILES):
+                sums = psum_t.tile([P, PACK, P], F32, name="sums", tag="t")
+                for c in range(P // CHUNK):
+                    for t in range(PACK):
+                        nc.tensor.matmul(
+                            out=sums[:, t, CHUNK * c : CHUNK * (c + 1)],
+                            lhsT=steps[:, (P // CHUNK) * i + c, t:D:PACK],
+                            rhs=same_row[:],
+                            start=True,
+                            stop=True,
                         )
+                sums_of[(n, VTILES + i)] = sums
+
+        def round_sums(n, tiles):
+            if ("pooled", n) not in grouped_of:
+                grouped = work.tile([P, GROUP, PACK], BF16, name="grouped_pooled", align_bytes=64)
+                grouped_of[("pooled", n)] = grouped
+            for i in tiles:
                 nc.scalar.copy(
-                    out=grouped_words[:, P * first : P * (first + count), :],
-                    in_=turned[:].rearrange("p u c -> p c u"),
+                    out=grouped_of[("pooled", n)][:, P * i : P * (i + 1), :],
+                    in_=sums_of[(n, i)][:].rearrange("p t c -> p c t"),
                 )
 
         def quantise(key):
@@ -185,50 +178,40 @@ def tile_semanticaligner_t_e_kernel(
             )
             return codes, planes
 
-        def turn_pooled(n):
-            turn_rows(pooled_of[n], VTILES, grouped_of[("pooled", n)])
-
         def quantise_pooled(n):
             pooled_mx[n] = quantise(("pooled", n))
 
         def hidden(n):
             m = n // GROUPS
             codes, planes = pooled_mx[n]
-            h_turned = work.tile([P, SLICES, GROUP], BF16, name="h_turned")
-            for j in range(SLICES):
+            z1_of[n] = []
+            for t in range(PACK):
                 z1 = psum_z1.tile([P, GROUP], F32, name="z1")
                 nc.tensor.matmul_mx(
                     out=z1[:],
-                    lhsT=w1_words[:, m, PACK * P * j : PACK * P * (j + 1)].bitcast(FP8X4),
-                    lhsT_scale=w1_planes[:, m, P * j : P * (j + 1)],
+                    lhsT=w1_words[:, m, t, :].bitcast(FP8X4),
+                    lhsT_scale=w1_planes[:, m, t, :],
                     rhs=codes[:].bitcast(FP8X4),
                     rhs_scale=planes[:],
                     start=True,
                     stop=True,
                 )
+                z1_of[n].append(z1)
+
+        def gelu(n, slices):
+            m = n // GROUPS
+            if n not in h_turned_of:
+                h_turned = work.tile([P, PACK, GROUP], BF16, name="h_turned")
+                h_turned_of[n] = h_turned
+            for t in slices:
                 nc.scalar.activation(
-                    out=h_turned[:, j, :], in_=z1[:], func=ACT.Gelu,
-                    bias=b1_cols[:, SLICES * m + j : SLICES * m + j + 1], scale=1.0 / STEPS,
+                    out=h_turned_of[n][:, t, :], in_=z1_of[n][t][:], func=ACT.Gelu,
+                    bias=b1_cols[:, PACK * m + t : PACK * m + t + 1], scale=1.0 / STEPS,
                 )
-            h_turned_of[n] = h_turned
 
-        def turn_back(n):
-            h_turned = h_turned_of[n]
-            h = work.tile([P, TILES, D], BF16, name="h")
-            for first in range(0, TILES, 2):
-                h_rows = psum_t.tile([P, 2, D], BF16, name="h_rows", tag="t")
-                for i in range(2):
-                    col = P * (first + i)
-                    for j in range(SLICES):
-                        nc.tensor.transpose(
-                            h_rows[:, i, P * j : P * (j + 1)], h_turned[:, j, col : col + P], ident_bf16[:]
-                        )
-                nc.scalar.copy(out=h[:, first : first + 2, :], in_=h_rows[:])
-            h_of[n] = h
-
-        def turn_h(n):
-            grouped = work.tile([P, GROUP, PACK], BF16, name="grouped", align_bytes=64)
-            turn_rows(h_of[n], TILES, grouped)
+        def group_h(n):
+            grouped = work.tile([P, GROUP, PACK], BF16, name="grouped_h", align_bytes=64)
+            nc.vector.tensor_copy(out=grouped[:], in_=h_turned_of[n][:].rearrange("p t c -> p c t"))
             grouped_of[("h", n)] = grouped
 
         def quantise_h(n):
@@ -250,20 +233,22 @@ def tile_semanticaligner_t_e_kernel(
                 )
             z_acc_of[n] = z_acc
 
-        def bias_and_mean(n):
+        def add_bias(n, tiles):
             m = n // GROUPS
-            z_acc = z_acc_of[n]
-            z = work.tile([P, TILES, PROJ], F32, name="z")
-            z_sum = work.tile([P, TILES], F32, name="z_sum")
-            for i in range(TILES):
+            if n not in z_of:
+                z = work.tile([P, TILES, PROJ], F32, name="z")
+                z_sum = work.tile([P, TILES], F32, name="z_sum")
+                z_of[n] = z
+                z_sum_of[n] = z_sum
+            for i in tiles:
                 nc.vector.scalar_tensor_tensor(
-                    out=z[:, i, :], in0=z_acc[:, i, :], scalar=1.0, in1=b2_all[:, m, :],
-                    op0=ALU.mult, op1=ALU.add, accum_out=z_sum[:, i : i + 1],
+                    out=z_of[n][:, i, :], in0=z_acc_of[n][:, i, :], scalar=1.0, in1=b2_all[:, m, :],
+                    op0=ALU.mult, op1=ALU.add, accum_out=z_sum_of[n][:, i : i + 1],
                 )
-            neg_mean = work.tile([P, TILES], F32, name="neg_mean")
-            nc.vector.tensor_scalar_mul(out=neg_mean[:], in0=z_sum[:], scalar1=-1.0 / PROJ)
-            z_of[n] = z
-            neg_mean_of[n] = neg_mean
+            if tiles[-1] == TILES - 1:
+                neg_mean = work.tile([P, TILES], F32, name="neg_mean")
+                nc.vector.tensor_scalar_mul(out=neg_mean[:], in0=z_sum_of[n][:], scalar1=-1.0 / PROJ)
+                neg_mean_of[n] = neg_mean
 
         def apply_gain(n):
             m = n // GROUPS
@@ -294,7 +279,7 @@ def tile_semanticaligner_t_e_kernel(
             nc.gpsimd.tensor_tensor(out=rstd[:], in0=var_eps[:], in1=minus_half[:], op=ALU.pow)
             rstd_of[n] = rstd
 
-        def shift_and_square(n):
+        def shift(n):
             m = n // GROUPS
             y = work.tile([P, TILES, PROJ], F32, name="y")
             for i in range(TILES):
@@ -302,13 +287,15 @@ def tile_semanticaligner_t_e_kernel(
                     out=y[:, i, :], in0=gained_of[n][:, i, :], scalar=rstd_of[n][:, i : i + 1],
                     in1=beta_all[:, m, :], op0=ALU.mult, op1=ALU.add,
                 )
+            y_of[n] = y
+
+        def square_y(n):
             y_squares = work.tile([P, TILES, PROJ], F32, name="y_squares")
             norm_sq = work.tile([P, TILES], F32, name="norm_sq")
             for i in range(TILES):
                 nc.scalar.activation(
-                    out=y_squares[:, i, :], in_=y[:, i, :], func=ACT.Square, accum_out=norm_sq[:, i : i + 1]
+                    out=y_squares[:, i, :], in_=y_of[n][:, i, :], func=ACT.Square, accum_out=norm_sq[:, i : i + 1]
                 )
-            y_of[n] = y
             norm_sq_of[n] = norm_sq
 
         def inverse_norm(n):
@@ -329,30 +316,35 @@ def tile_semanticaligner_t_e_kernel(
             nc.scalar.dma_start(
                 out=rows[0:VROWS].rearrange("(p i) c -> p i c", i=VTILES), in_=result[:, 0:VTILES, :]
             )
-            nc.scalar.dma_start(out=rows[VROWS:GROUP], in_=result[:, VTILES, :])
+            nc.scalar.dma_start(
+                out=rows[VROWS:GROUP].rearrange("(i p) c -> p i c", p=P), in_=result[:, VTILES:TILES, :]
+            )
 
         def run(stage, n, *args):
             if 0 <= n < TOTAL:
                 stage(n, *args)
 
-        for n in range(-2, TOTAL + 2):
+        for n in range(-2, TOTAL + 3):
+            run(gelu, n, (0, 1, 2, 3))
+            run(turn_pairs, n + 1)
+            run(inverse_std, n - 2)
+            run(add_bias, n - 1, (0, 1))
+            run(add_pairs, n + 2, 0)
+            run(round_sums, n + 1, (0, 1))
+            run(add_steps, n + 2)
+            run(shift, n - 2)
+            run(square_y, n - 2)
+            run(group_h, n)
+            run(quantise_pooled, n + 1)
+            run(hidden, n + 1)
+            run(round_sums, n + 2, (2, 3))
             run(inverse_norm, n - 2)
-            run(bias_and_mean, n - 1)
+            run(add_bias, n - 1, (2, 3))
+            run(quantise_h, n)
+            run(project, n)
+            run(finish, n - 2)
             run(apply_gain, n - 1)
             run(square_deviations, n - 1)
-            run(add_pairs, n + 2, 0)
-            run(inverse_std, n - 1)
-            run(round_steps, n + 1)
-            run(turn_back, n)
-            run(finish, n - 2)
             run(add_pairs, n + 2, 1)
-            run(turn_pooled, n + 1)
-            run(turn_h, n)
-            run(shift_and_square, n - 1)
-            run(quantise_pooled, n + 1)
-            run(add_halves, n + 2, 0)
-            run(quantise_h, n)
-            run(hidden, n + 1)
-            run(project, n)
-            run(add_steps, n + 2)
-            run(add_halves, n + 2, 1)
+            if n + 6 < TOTAL:
+                load(n + 6)

@@ -146,23 +146,29 @@ def tile_semanticaligner_t_e_kernel(
 
         def add_steps(n):
             steps = steps_of[n]
+            sums = psum_t.tile([P, TILES - VTILES, PACK, P], BF16, name="sums_bf16", tag="t")
+            sums_of[(n, "tensor")] = sums
             for i in range(TILES - VTILES):
-                sums = psum_t.tile([P, PACK, P], F32, name="sums", tag="t")
                 for c in range(P // CHUNK):
                     for t in range(PACK):
                         nc.tensor.matmul(
-                            out=sums[:, t, CHUNK * c : CHUNK * (c + 1)],
+                            out=sums[:, i, t, CHUNK * c : CHUNK * (c + 1)],
                             lhsT=steps[:, (P // CHUNK) * i + c, t:D:PACK],
                             rhs=same_row[:],
                             start=True,
                             stop=True,
                         )
-                sums_of[(n, VTILES + i)] = sums
 
         def round_sums(n, tiles):
             if ("pooled", n) not in grouped_of:
                 grouped = work.tile([P, GROUP, PACK], BF16, name="grouped_pooled", align_bytes=64)
                 grouped_of[("pooled", n)] = grouped
+            if tiles == "tensor":
+                nc.scalar.copy(
+                    out=grouped_of[("pooled", n)][:, VROWS:GROUP, :].rearrange("p (i c) t -> p i c t", c=P),
+                    in_=sums_of[(n, "tensor")][:].rearrange("p i t c -> p i c t"),
+                )
+                return
             for i in tiles:
                 nc.scalar.copy(
                     out=grouped_of[("pooled", n)][:, P * i : P * (i + 1), :],
@@ -337,7 +343,7 @@ def tile_semanticaligner_t_e_kernel(
             run(group_h, n)
             run(quantise_pooled, n + 1)
             run(hidden, n + 1)
-            run(round_sums, n + 2, (2, 3))
+            run(round_sums, n + 2, "tensor")
             run(inverse_norm, n - 2)
             run(add_bias, n - 1, (2, 3))
             run(quantise_h, n)

@@ -128,9 +128,9 @@ def tile_semanticaligner_t_e_kernel(
         nc.vector.tensor_copy(out=b1_cols[:], in_=b1_raw[:].rearrange("p m t -> p (m t)"))
 
         def add_pairs(n, i):
-            pairs = work.tile([P, 2, D], F32, name="pairs", bufs=4)
-            x_pairs = x_of[n][:].rearrange("p i (h e) d -> p i h e d", e=2)
-            nc.vector.tensor_tensor(out=pairs[:], in0=x_pairs[:, i, :, 0, :], in1=x_pairs[:, i, :, 1, :], op=ALU.add)
+            pairs = work.tile([P, 2, PACK, P], F32, name="pairs", bufs=4)
+            x_pairs = x_of[n][:].rearrange("p i (h e) (j t) -> p i h e t j", e=2, t=PACK)
+            nc.vector.tensor_tensor(out=pairs[:], in0=x_pairs[:, i, :, 0], in1=x_pairs[:, i, :, 1], op=ALU.add)
             pairs_of[(n, i)] = pairs
 
         def turn_pairs(n):
@@ -139,7 +139,7 @@ def tile_semanticaligner_t_e_kernel(
                 for t in range(PACK):
                     for h in range(2):
                         nc.tensor.matmul(
-                            out=sums[:, t, :], lhsT=pairs_of[(n, i)][:, h, t:D:PACK], rhs=ident_f32[:],
+                            out=sums[:, t, :], lhsT=pairs_of[(n, i)][:, h, t, :], rhs=ident_f32[:],
                             is_transpose=True, start=(h == 0), stop=(h == 1),
                         )
                 sums_of[(n, i)] = sums

@@ -68,7 +68,7 @@ def tile_semanticaligner_t_e_kernel(
         w2_planes = consts.tile([P, MODS, PROJ], U8, align_bytes=64)
         nc.vector.memset(w1_planes_raw[:].bitcast(I32), 0)
         nc.vector.memset(w2_planes[:].bitcast(I32), 0)
-        minus_half = consts.tile([P, TILES], F32)
+        minus_half = consts.tile([P, 2 * TILES], F32)
         nc.vector.memset(minus_half[:], -0.5)
         warm = consts.tile([P, 1], F32)
         nc.scalar.activation(out=warm[:], in_=minus_half[:, 0:1], func=ACT.Gelu)
@@ -276,14 +276,25 @@ def tile_semanticaligner_t_e_kernel(
                 )
             dev_sum_of[n] = dev_sum
 
-        def inverse_std(n):
-            var_eps = work.tile([P, TILES], F32, name="var_eps")
-            nc.vector.tensor_scalar(
-                out=var_eps[:], in0=dev_sum_of[n][:], scalar1=1.0 / PROJ, scalar2=LN_EPS, op0=ALU.mult, op1=ALU.add
-            )
-            rstd = work.tile([P, TILES], F32, name="rstd")
-            nc.gpsimd.tensor_tensor(out=rstd[:], in0=var_eps[:], in1=minus_half[:], op=ALU.pow)
-            rstd_of[n] = rstd
+        def inverse_roots(n_std, n_norm):
+            has_std, has_norm = 0 <= n_std < TOTAL, 0 <= n_norm < TOTAL
+            if not (has_std or has_norm):
+                return
+            radicands = work.tile([P, 2 * TILES], F32, name="radicands")
+            roots = work.tile([P, 2 * TILES], F32, name="roots")
+            if has_std:
+                nc.vector.tensor_scalar(
+                    out=radicands[:, 0:TILES], in0=dev_sum_of[n_std][:], scalar1=1.0 / PROJ, scalar2=LN_EPS,
+                    op0=ALU.mult, op1=ALU.add,
+                )
+                rstd_of[n_std] = roots[:, 0:TILES]
+            if has_norm:
+                nc.vector.tensor_scalar_max(
+                    out=radicands[:, TILES : 2 * TILES], in0=norm_sq_of[n_norm][:], scalar1=NORM_EPS * NORM_EPS
+                )
+                inv_norm_of[n_norm] = roots[:, TILES : 2 * TILES]
+            cols = slice(0 if has_std else TILES, 2 * TILES if has_norm else TILES)
+            nc.gpsimd.tensor_tensor(out=roots[:, cols], in0=radicands[:, cols], in1=minus_half[:, cols], op=ALU.pow)
 
         def shift(n):
             m = n // GROUPS
@@ -304,13 +315,6 @@ def tile_semanticaligner_t_e_kernel(
                 )
             norm_sq_of[n] = norm_sq
 
-        def inverse_norm(n):
-            norm_floor = work.tile([P, TILES], F32, name="norm_floor")
-            nc.vector.tensor_scalar_max(out=norm_floor[:], in0=norm_sq_of[n][:], scalar1=NORM_EPS * NORM_EPS)
-            inv_norm = work.tile([P, TILES], F32, name="inv_norm")
-            nc.gpsimd.tensor_tensor(out=inv_norm[:], in0=norm_floor[:], in1=minus_half[:], op=ALU.pow)
-            inv_norm_of[n] = inv_norm
-
         def finish(n):
             m, g = divmod(n, GROUPS)
             result = work.tile([P, TILES, PROJ], F32, name="result")
@@ -330,27 +334,25 @@ def tile_semanticaligner_t_e_kernel(
             if 0 <= n < TOTAL:
                 stage(n, *args)
 
-        for n in range(-2, TOTAL + 3):
+        for n in range(-2, TOTAL + 4):
             run(gelu, n, (0, 1, 2, 3))
             run(turn_pairs, n + 1)
-            run(inverse_std, n - 2)
-            run(add_bias, n - 1, (0, 1))
+            inverse_roots(n - 2, n - 3)
+            run(add_bias, n - 1, (0, 1, 2, 3))
             run(add_pairs, n + 2, 0)
             run(round_sums, n + 1, (0, 1))
             run(add_steps, n + 2)
+            run(finish, n - 3)
             run(shift, n - 2)
-            run(square_y, n - 2)
+            run(square_deviations, n - 1)
             run(group_h, n)
+            run(square_y, n - 2)
             run(quantise_pooled, n + 1)
             run(hidden, n + 1)
             run(round_sums, n + 2, "tensor")
-            run(inverse_norm, n - 2)
-            run(add_bias, n - 1, (2, 3))
             run(quantise_h, n)
             run(project, n)
-            run(finish, n - 2)
             run(apply_gain, n - 1)
-            run(square_deviations, n - 1)
             run(add_pairs, n + 2, 1)
             if n + 6 < TOTAL:
                 load(n + 6)

@@ -27,6 +27,7 @@ VTILES = 2
 VROWS = VTILES * P
 CHUNK = P // STEPS
 CHUNKS = (GROUP - VROWS) // CHUNK
+SCALAR_COLS = 128
 LN_EPS = 1e-5
 NORM_EPS = 1e-12
 
@@ -217,7 +218,9 @@ def tile_semanticaligner_t_e_kernel(
 
         def group_h(n):
             grouped = work.tile([P, GROUP, PACK], BF16, name="grouped_h", align_bytes=64)
-            nc.vector.tensor_copy(out=grouped[:], in_=h_turned_of[n][:].rearrange("p t c -> p c t"))
+            turned = h_turned_of[n][:].rearrange("p t c -> p c t")
+            nc.scalar.copy(out=grouped[:, 0:SCALAR_COLS, :], in_=turned[:, 0:SCALAR_COLS, :])
+            nc.vector.tensor_copy(out=grouped[:, SCALAR_COLS:GROUP, :], in_=turned[:, SCALAR_COLS:GROUP, :])
             grouped_of[("h", n)] = grouped
 
         def quantise_h(n):

@@ -28,6 +28,7 @@ VROWS = VTILES * P
 CHUNK = P // STEPS
 CHUNKS = (GROUP - VROWS) // CHUNK
 SCALAR_COLS = 128
+RUN = 4
 LN_EPS = 1e-5
 NORM_EPS = 1e-12
 
@@ -218,9 +219,11 @@ def tile_semanticaligner_t_e_kernel(
 
         def group_h(n):
             grouped = work.tile([P, GROUP, PACK], BF16, name="grouped_h", align_bytes=64)
-            turned = h_turned_of[n][:].rearrange("p t c -> p c t")
-            nc.scalar.copy(out=grouped[:, 0:SCALAR_COLS, :], in_=turned[:, 0:SCALAR_COLS, :])
-            nc.vector.tensor_copy(out=grouped[:, SCALAR_COLS:GROUP, :], in_=turned[:, SCALAR_COLS:GROUP, :])
+            turned = h_turned_of[n][:].rearrange("p t (c i) -> p c t i", i=RUN)
+            laid = grouped[:].rearrange("p (c i) t -> p c t i", i=RUN)
+            cut = SCALAR_COLS // RUN
+            nc.scalar.copy(out=laid[:, 0:cut], in_=turned[:, 0:cut])
+            nc.vector.tensor_copy(out=laid[:, cut:], in_=turned[:, cut:])
             grouped_of[("h", n)] = grouped
 
         def quantise_h(n):

@@ -59,12 +59,14 @@ def tile_semanticaligner_t_e_kernel(
                 return
             m, g = divmod(n, GROUPS)
             rows = feats[m, GROUP * g : GROUP * (g + 1)]
-            x = loads.tile([P, VTILES, STEPS, D], BF16, name="x")
-            nc.sync.dma_start(out=x[:], in_=rows[0:VROWS].rearrange("(p i) t d -> p i t d", i=VTILES))
-            x_of[n] = x
             steps = loads.tile([P, CHUNKS, D], BF16, name="steps")
             nc.sync.dma_start(out=steps[:], in_=rows[VROWS:GROUP].rearrange("(c l) t d -> (l t) c d", l=CHUNK))
             steps_of[n] = steps
+            x = loads.tile([P, VTILES, STEPS, D], BF16, name="x")
+            v_rows = rows[0:VROWS].rearrange("(p i) t d -> p i t d", i=VTILES)
+            for i in range(VTILES):
+                nc.sync.dma_start(out=x[:, i], in_=v_rows[:, i])
+            x_of[n] = x
 
         w1_planes_raw = consts.tile([P, MODS, D], U8, align_bytes=64)
         w2_planes = consts.tile([P, MODS, PROJ], U8, align_bytes=64)
@@ -75,17 +77,19 @@ def tile_semanticaligner_t_e_kernel(
         warm = consts.tile([P, 1], F32)
         nc.scalar.activation(out=warm[:], in_=minus_half[:, 0:1], func=ACT.Gelu)
 
+        load(0)
         for quad in range(4):
             nc.sync.dma_start(
                 out=w1_planes_raw[32 * quad : 32 * quad + 4].bitcast(I32),
                 in_=W1_scales[:, 4 * quad : 4 * quad + 4, :].rearrange("g r n -> r g n").bitcast(I32),
             )
         w1_words_raw = consts.tile([P, MODS, D], I32)
-        nc.sync.dma_start(out=w1_words_raw[:], in_=W1_words.rearrange("g p n t -> p g (n t)").bitcast(I32))
-        load(0)
+        w1_source = W1_words.rearrange("g p n t -> p g (n t)").bitcast(I32)
+        nc.sync.dma_start(out=w1_words_raw[:, 0, :], in_=w1_source[:, 0, :])
         b1_raw = consts.tile([P, MODS, PACK], BF16)
         nc.sync.dma_start(out=b1_raw[:], in_=b1.rearrange("m (p t) -> p m t", t=PACK))
         load(1)
+        nc.sync.dma_start(out=w1_words_raw[:, 1:MODS, :], in_=w1_source[:, 1:MODS, :])
         for quad in range(4):
             nc.sync.dma_start(
                 out=w2_planes[32 * quad : 32 * quad + 4].bitcast(I32),
@@ -118,7 +122,9 @@ def tile_semanticaligner_t_e_kernel(
 
         w1_words = consts.tile([P, MODS, PACK, P], I32, align_bytes=64)
         w1_planes = consts.tile([P, MODS, PACK, P], U8, align_bytes=64)
-        for m in range(MODS):
+        b1_cols = consts.tile([P, MODS * PACK], F32)
+
+        def regroup_w1(m):
             nc.vector.tensor_copy(
                 out=w1_words[:, m, :, :], in_=w1_words_raw[:, m, :].rearrange("p (j t) -> p t j", t=PACK)
             )
@@ -126,8 +132,8 @@ def tile_semanticaligner_t_e_kernel(
                 out=w1_planes[:, m, :, :].rearrange("p t j -> p j t"),
                 in_=w1_planes_raw[:, m, :].rearrange("p (j t) -> p j t", t=PACK),
             )
-        b1_cols = consts.tile([P, MODS * PACK], F32)
-        nc.vector.tensor_copy(out=b1_cols[:], in_=b1_raw[:].rearrange("p m t -> p (m t)"))
+            if m == 0:
+                nc.vector.tensor_copy(out=b1_cols[:], in_=b1_raw[:].rearrange("p m t -> p (m t)"))
 
         def add_pairs(n, i):
             pairs = work.tile([P, 2, PACK, P], F32, name="pairs", bufs=4)
@@ -345,20 +351,25 @@ def tile_semanticaligner_t_e_kernel(
             run(turn_pairs, n + 1)
             inverse_roots(n - 2, n - 3)
             run(add_bias, n - 1, (0, 1, 2, 3))
-            run(add_pairs, n + 2, 0)
+            if n >= 1:
+                run(add_pairs, n + 2, 0)
             run(round_sums, n + 1, (0, 1))
             run(add_steps, n + 2)
             run(finish, n - 3)
             run(shift, n - 2)
             run(square_deviations, n - 1)
-            run(group_h, n)
-            run(square_y, n - 2)
             run(quantise_pooled, n + 1)
             run(hidden, n + 1)
+            run(group_h, n)
+            run(square_y, n - 2)
             run(round_sums, n + 2, "tensor")
+            run(apply_gain, n - 1)
             run(quantise_h, n)
             run(project, n)
-            run(apply_gain, n - 1)
+            if n < 1:
+                run(add_pairs, n + 2, 0)
             run(add_pairs, n + 2, 1)
+            if n + 2 < MODS:
+                regroup_w1(n + 2)
             if n + 6 < TOTAL:
                 load(n + 6)

@@ -1,3 +1,4 @@
+import math
 from contextlib import ExitStack
 
 import concourse.mybir as mybir
@@ -51,7 +52,7 @@ def tile_semanticaligner_t_e_kernel(
         x_of, steps_of, sums_of, pairs_of, pooled_of, turned_of, pooled_mx, z1_of, h_turned_of, h_mx = (
             {}, {}, {}, {}, {}, {}, {}, {}, {}, {}
         )
-        z_acc_of, dev_sum_of, z_sum_of = {}, {}, {}
+        z_acc_of, square_sums_of, z_sum_of = {}, {}, {}
         grouped_of, z_of, neg_mean_of, rstd_of, gained_of, y_of, norm_sq_of, inv_norm_of = {}, {}, {}, {}, {}, {}, {}, {}
 
         def load(n):
@@ -110,6 +111,10 @@ def tile_semanticaligner_t_e_kernel(
         load(2)
         load(3)
 
+        gamma_scaled = consts.tile([P, MODS, PROJ], F32)
+        floors = consts.tile([P, 2 * TILES], F32)
+        nc.vector.memset(floors[:], 0.0)
+        nc.vector.tensor_scalar_add(out=floors[:, 0:TILES], in0=floors[:, TILES : 2 * TILES], scalar1=PROJ * LN_EPS)
         ident_f32 = consts.tile([P, P], F32)
         make_identity(nc, ident_f32[:])
         same_row_f32 = consts.tile([P, CHUNK], F32)
@@ -274,39 +279,40 @@ def tile_semanticaligner_t_e_kernel(
             for i in range(TILES):
                 nc.vector.scalar_tensor_tensor(
                     out=gained[:, i, :], in0=z_of[n][:, i, :], scalar=neg_mean_of[n][:, i : i + 1],
-                    in1=gamma_all[:, m, :], op0=ALU.add, op1=ALU.mult,
+                    in1=gamma_scaled[:, m, :], op0=ALU.add, op1=ALU.mult,
                 )
             gained_of[n] = gained
 
+        def square_sums(r):
+            if r not in square_sums_of:
+                sums = work.tile([P, 2 * TILES], F32, name="square_sums")
+                square_sums_of[r] = sums
+            return square_sums_of[r]
+
         def square_deviations(n):
             squares = work.tile([P, TILES, PROJ], F32, name="squares")
-            dev_sum = work.tile([P, TILES], F32, name="dev_sum")
+            dev_sum = square_sums(n + 1)[:, 0:TILES]
             for i in range(TILES):
                 nc.scalar.activation(
                     out=squares[:, i, :], in_=z_of[n][:, i, :], func=ACT.Square,
                     bias=neg_mean_of[n][:, i : i + 1], scale=1.0, accum_out=dev_sum[:, i : i + 1],
                 )
-            dev_sum_of[n] = dev_sum
 
         def inverse_roots(n_std, n_norm):
             has_std, has_norm = 0 <= n_std < TOTAL, 0 <= n_norm < TOTAL
             if not (has_std or has_norm):
                 return
+            cols = slice(0 if has_std else TILES, 2 * TILES if has_norm else TILES)
+            sums = square_sums_of[n_std + 1]
             radicands = work.tile([P, 2 * TILES], F32, name="radicands")
             roots = work.tile([P, 2 * TILES], F32, name="roots")
-            if has_std:
-                nc.vector.tensor_scalar(
-                    out=radicands[:, 0:TILES], in0=dev_sum_of[n_std][:], scalar1=1.0 / PROJ, scalar2=LN_EPS,
-                    op0=ALU.mult, op1=ALU.add,
-                )
-                rstd_of[n_std] = roots[:, 0:TILES]
-            if has_norm:
-                nc.vector.tensor_scalar_max(
-                    out=radicands[:, TILES : 2 * TILES], in0=norm_sq_of[n_norm][:], scalar1=NORM_EPS * NORM_EPS
-                )
-                inv_norm_of[n_norm] = roots[:, TILES : 2 * TILES]
-            cols = slice(0 if has_std else TILES, 2 * TILES if has_norm else TILES)
+            nc.vector.scalar_tensor_tensor(
+                out=radicands[:, cols], in0=sums[:, cols], scalar=NORM_EPS * NORM_EPS, in1=floors[:, cols],
+                op0=ALU.max, op1=ALU.add,
+            )
             nc.gpsimd.tensor_tensor(out=roots[:, cols], in0=radicands[:, cols], in1=minus_half[:, cols], op=ALU.pow)
+            rstd_of[n_std] = roots[:, 0:TILES]
+            inv_norm_of[n_norm] = roots[:, TILES : 2 * TILES]
 
         def shift(n):
             m = n // GROUPS
@@ -320,12 +326,11 @@ def tile_semanticaligner_t_e_kernel(
 
         def square_y(n):
             y_squares = work.tile([P, TILES, PROJ], F32, name="y_squares")
-            norm_sq = work.tile([P, TILES], F32, name="norm_sq")
+            norm_sq = square_sums(n + 2)[:, TILES : 2 * TILES]
             for i in range(TILES):
                 nc.scalar.activation(
                     out=y_squares[:, i, :], in_=y_of[n][:, i, :], func=ACT.Square, accum_out=norm_sq[:, i : i + 1]
                 )
-            norm_sq_of[n] = norm_sq
 
         def finish(n):
             m, g = divmod(n, GROUPS)
@@ -335,10 +340,10 @@ def tile_semanticaligner_t_e_kernel(
                     out=result[:, i, :], in_=y_of[n][:, i, :], func=ACT.Copy, scale=inv_norm_of[n][:, i : i + 1]
                 )
             rows = out[m, GROUP * g : GROUP * (g + 1), :]
-            nc.scalar.dma_start(
+            nc.sync.dma_start(
                 out=rows[0:VROWS].rearrange("(p i) c -> p i c", i=VTILES), in_=result[:, 0:VTILES, :]
             )
-            nc.scalar.dma_start(
+            nc.sync.dma_start(
                 out=rows[VROWS:GROUP].rearrange("(i p) c -> p i c", p=P), in_=result[:, VTILES:TILES, :]
             )
 
@@ -371,5 +376,7 @@ def tile_semanticaligner_t_e_kernel(
             run(add_pairs, n + 2, 1)
             if n + 2 < MODS:
                 regroup_w1(n + 2)
+            if n == 0:
+                nc.vector.tensor_scalar_mul(out=gamma_scaled[:], in0=gamma_all[:], scalar1=math.sqrt(PROJ))
             if n + 6 < TOTAL:
                 load(n + 6)

import math
from contextlib import ExitStack

import concourse.mybir as mybir
from concourse.masks import make_identity

F32 = mybir.dt.float32
BF16 = mybir.dt.bfloat16
I32 = mybir.dt.int32
U32 = mybir.dt.uint32
U8 = mybir.dt.uint8
FP8X4 = mybir.dt.float8_e4m3fn_x4
ALU = mybir.AluOpType
ACT = mybir.ActivationFunctionType

P = 128
PACK = 4
MODS = 3
BATCH = 2048
STEPS = 4
D = 512
PROJ = 128
TILES = 4
GROUP = TILES * P
GROUPS = BATCH // GROUP
TOTAL = MODS * GROUPS
VTILES = 2
VROWS = VTILES * P
CHUNK = P // STEPS
CHUNKS = (GROUP - VROWS) // CHUNK
SCALAR_COLS = 128
RUN = 4
LN_EPS = 1e-5
NORM_EPS = 1e-12

FLOPS = 2 * MODS * BATCH * (D * D + D * PROJ)


def tile_semanticaligner_t_e_kernel(
    tc, feats, W1_words, W1_scales, b1, W2_words, W2_scales, b2, gamma, beta, out
):
    nc = tc.nc
    with ExitStack() as ctx:
        ctx.enter_context(tc.manual_schedule())
        consts = ctx.enter_context(tc.tile_pool(name="consts", bufs=1))
        loads = ctx.enter_context(tc.tile_pool(name="loads", bufs=4))
        work = ctx.enter_context(tc.tile_pool(name="work", bufs=3))
        psum_t = ctx.enter_context(tc.psum_pool(name="psum_t", bufs=3))
        psum_z1 = ctx.enter_context(tc.psum_pool(name="psum_z1", bufs=4))
        psum_z = ctx.enter_context(tc.psum_pool(name="psum_z", bufs=1))

        x_of, steps_of, sums_of, pairs_of, pooled_of, turned_of, pooled_mx, z1_of, h_turned_of, h_mx = (
            {}, {}, {}, {}, {}, {}, {}, {}, {}, {}
        )
        z_acc_of, square_sums_of, z_sum_of = {}, {}, {}
        grouped_of, z_of, neg_mean_of, rstd_of, gained_of, y_of, norm_sq_of, inv_norm_of = {}, {}, {}, {}, {}, {}, {}, {}

        def load(n):
            if n >= TOTAL:
                return
            m, g = divmod(n, GROUPS)
            rows = feats[m, GROUP * g : GROUP * (g + 1)]
            steps = loads.tile([P, CHUNKS, D], BF16, name="steps")
            nc.sync.dma_start(out=steps[:], in_=rows[VROWS:GROUP].rearrange("(c l) t d -> (l t) c d", l=CHUNK))
            steps_of[n] = steps
            x = loads.tile([P, VTILES, STEPS, D], BF16, name="x")
            v_rows = rows[0:VROWS].rearrange("(p i) t d -> p i t d", i=VTILES)
            for i in range(VTILES):
                nc.sync.dma_start(out=x[:, i], in_=v_rows[:, i])
            x_of[n] = x

        w1_planes_raw = consts.tile([P, MODS, D], U8, align_bytes=64)
        w2_planes = consts.tile([P, MODS, PROJ], U8, align_bytes=64)
        nc.vector.memset(w1_planes_raw[:].bitcast(I32), 0)
        nc.vector.memset(w2_planes[:].bitcast(I32), 0)
        minus_half = consts.tile([P, 2 * TILES], F32)
        nc.vector.memset(minus_half[:], -0.5)
        warm = consts.tile([P, 1], F32)
        nc.scalar.activation(out=warm[:], in_=minus_half[:, 0:1], func=ACT.Gelu)

        load(0)
        for quad in range(4):
            nc.sync.dma_start(
                out=w1_planes_raw[32 * quad : 32 * quad + 4].bitcast(I32),
                in_=W1_scales[:, 4 * quad : 4 * quad + 4, :].rearrange("g r n -> r g n").bitcast(I32),
            )
        w1_words_raw = consts.tile([P, MODS, D], I32)
        w1_source = W1_words.rearrange("g p n t -> p g (n t)").bitcast(I32)
        nc.sync.dma_start(out=w1_words_raw[:, 0, :], in_=w1_source[:, 0, :])
        b1_raw = consts.tile([P, MODS, PACK], BF16)
        nc.sync.dma_start(out=b1_raw[:], in_=b1.rearrange("m (p t) -> p m t", t=PACK))
        load(1)
        nc.sync.dma_start(out=w1_words_raw[:, 1:MODS, :], in_=w1_source[:, 1:MODS, :])
        for quad in range(4):
            nc.sync.dma_start(
                out=w2_planes[32 * quad : 32 * quad + 4].bitcast(I32),
                in_=W2_scales[:, 4 * quad : 4 * quad + 4, :].rearrange("g r n -> r g n").bitcast(I32),
            )
        w2_words = consts.tile([P, MODS, PACK * PROJ], U8, align_bytes=64)
        nc.sync.dma_start(
            out=w2_words[:].bitcast(I32), in_=W2_words.rearrange("g p n t -> p g (n t)").bitcast(I32)
        )
        b2_all = consts.tile([P, MODS, PROJ], BF16)
        gamma_all = consts.tile([P, MODS, PROJ], BF16)
        beta_all = consts.tile([P, MODS, PROJ], BF16)
        for row_tile, vec in ((b2_all, b2), (gamma_all, gamma), (beta_all, beta)):
            nc.sync.dma_start(
                out=row_tile[:].rearrange("p m c -> p (m c)"),
                in_=vec.rearrange("m c -> (m c)").partition_broadcast(P),
            )
        load(2)
        load(3)

        gamma_scaled = consts.tile([P, MODS, PROJ], F32)
        floors = consts.tile([P, 2 * TILES], F32)
        nc.vector.memset(floors[:], 0.0)
        nc.vector.tensor_scalar_add(out=floors[:, 0:TILES], in0=floors[:, TILES : 2 * TILES], scalar1=PROJ * LN_EPS)
        ident_f32 = consts.tile([P, P], F32)
        make_identity(nc, ident_f32[:])
        same_row_f32 = consts.tile([P, CHUNK], F32)
        nc.vector.tensor_reduce(
            out=same_row_f32[:], in_=ident_f32[:].rearrange("p (l t) -> p l t", t=STEPS),
            axis=mybir.AxisListType.X, op=ALU.add,
        )
        same_row = consts.tile([P, CHUNK], BF16)
        nc.vector.tensor_copy(out=same_row[:], in_=same_row_f32[:])

        w1_words = consts.tile([P, MODS, PACK, P], I32, align_bytes=64)
        w1_planes = consts.tile([P, MODS, PACK, P], U8, align_bytes=64)
        b1_cols = consts.tile([P, MODS * PACK], F32)

        def regroup_w1(m):
            nc.vector.tensor_copy(
                out=w1_words[:, m, :, :], in_=w1_words_raw[:, m, :].rearrange("p (j t) -> p t j", t=PACK)
            )
            nc.vector.tensor_copy(
                out=w1_planes[:, m, :, :].rearrange("p t j -> p j t"),
                in_=w1_planes_raw[:, m, :].rearrange("p (j t) -> p j t", t=PACK),
            )
            if m == 0:
                nc.vector.tensor_copy(out=b1_cols[:], in_=b1_raw[:].rearrange("p m t -> p (m t)"))

        def add_pairs(n, i):
            pairs = work.tile([P, 2, PACK, P], F32, name="pairs", bufs=4)
            x_pairs = x_of[n][:].rearrange("p i (h e) (j t) -> p i h e t j", e=2, t=PACK)
            nc.vector.tensor_tensor(out=pairs[:], in0=x_pairs[:, i, :, 0], in1=x_pairs[:, i, :, 1], op=ALU.add)
            pairs_of[(n, i)] = pairs

        def turn_pairs(n):
            for i in range(VTILES):
                sums = psum_t.tile([P, PACK, P], F32, name="sums", tag="t")
                for t in range(PACK):
                    for h in range(2):
                        nc.tensor.matmul(
                            out=sums[:, t, :], lhsT=pairs_of[(n, i)][:, h, t, :], rhs=ident_f32[:],
                            is_transpose=True, start=(h == 0), stop=(h == 1),
                        )
                sums_of[(n, i)] = sums

        def add_steps(n):
            steps = steps_of[n]
            sums = psum_t.tile([P, TILES - VTILES, PACK, P], BF16, name="sums_bf16", tag="t")
            sums_of[(n, "tensor")] = sums
            for i in range(TILES - VTILES):
                for c in range(P // CHUNK):
                    for t in range(PACK):
                        nc.tensor.matmul(
                            out=sums[:, i, t, CHUNK * c : CHUNK * (c + 1)],
                            lhsT=steps[:, (P // CHUNK) * i + c, t:D:PACK],
                            rhs=same_row[:],
                            start=True,
                            stop=True,
                        )

        def round_sums(n, tiles):
            if ("pooled", n) not in grouped_of:
                grouped = work.tile([P, GROUP, PACK], BF16, name="grouped_pooled", align_bytes=64)
                grouped_of[("pooled", n)] = grouped
            if tiles == "tensor":
                nc.scalar.copy(
                    out=grouped_of[("pooled", n)][:, VROWS:GROUP, :].rearrange("p (i c) t -> p i c t", c=P),
                    in_=sums_of[(n, "tensor")][:].rearrange("p i t c -> p i c t"),
                )
                return
            for i in tiles:
                nc.scalar.copy(
                    out=grouped_of[("pooled", n)][:, P * i : P * (i + 1), :],
                    in_=sums_of[(n, i)][:].rearrange("p t c -> p c t"),
                )

        def quantise(key):
            codes = work.tile([P, GROUP], U32, name="codes", align_bytes=64)
            planes = work.tile([P, GROUP], U8, name="planes", align_bytes=64)
            nc.vector.quantize_mx(
                out=codes[:].bitcast(FP8X4), scales=planes[:],
                in_=grouped_of[key][:].rearrange("p c t -> p (c t)"),
            )
            return codes, planes

        def quantise_pooled(n):
            pooled_mx[n] = quantise(("pooled", n))

        def hidden(n):
            m = n // GROUPS
            codes, planes = pooled_mx[n]
            z1_of[n] = []
            for t in range(PACK):
                z1 = psum_z1.tile([P, GROUP], F32, name="z1")
                nc.tensor.matmul_mx(
                    out=z1[:],
                    lhsT=w1_words[:, m, t, :].bitcast(FP8X4),
                    lhsT_scale=w1_planes[:, m, t, :],
                    rhs=codes[:].bitcast(FP8X4),
                    rhs_scale=planes[:],
                    start=True,
                    stop=True,
                )
                z1_of[n].append(z1)

        def gelu(n, slices):
            m = n // GROUPS
            if n not in h_turned_of:
                h_turned = work.tile([P, PACK, GROUP], BF16, name="h_turned")
                h_turned_of[n] = h_turned
            for t in slices:
                nc.scalar.activation(
                    out=h_turned_of[n][:, t, :], in_=z1_of[n][t][:], func=ACT.Gelu,
                    bias=b1_cols[:, PACK * m + t : PACK * m + t + 1], scale=1.0 / STEPS,
                )

        def group_h(n):
            grouped = work.tile([P, GROUP, PACK], BF16, name="grouped_h", align_bytes=64)
            turned = h_turned_of[n][:].rearrange("p t (c i) -> p c t i", i=RUN)
            laid = grouped[:].rearrange("p (c i) t -> p c t i", i=RUN)
            cut = SCALAR_COLS // RUN
            nc.scalar.copy(out=laid[:, 0:cut], in_=turned[:, 0:cut])
            nc.vector.tensor_copy(out=laid[:, cut:], in_=turned[:, cut:])
            grouped_of[("h", n)] = grouped

        def quantise_h(n):
            h_mx[n] = quantise(("h", n))

        def project(n):
            m = n // GROUPS
            codes, planes = h_mx[n]
            z_acc = psum_z.tile([P, TILES, PROJ], F32, name="z_acc")
            for i in range(TILES):
                nc.tensor.matmul_mx(
                    out=z_acc[:, i, :],
                    lhsT=codes[:, P * i : P * (i + 1)].bitcast(FP8X4),
                    lhsT_scale=planes[:, P * i : P * (i + 1)],
                    rhs=w2_words[:, m, :].bitcast(FP8X4),
                    rhs_scale=w2_planes[:, m, :],
                    start=True,
                    stop=True,
                )
            z_acc_of[n] = z_acc

        def add_bias(n, tiles):
            m = n // GROUPS
            if n not in z_of:
                z = work.tile([P, TILES, PROJ], F32, name="z")
                z_sum = work.tile([P, TILES], F32, name="z_sum")
                z_of[n] = z
                z_sum_of[n] = z_sum
            for i in tiles:
                nc.vector.scalar_tensor_tensor(
                    out=z_of[n][:, i, :], in0=z_acc_of[n][:, i, :], scalar=1.0, in1=b2_all[:, m, :],
                    op0=ALU.mult, op1=ALU.add, accum_out=z_sum_of[n][:, i : i + 1],
                )
            if tiles[-1] == TILES - 1:
                neg_mean = work.tile([P, TILES], F32, name="neg_mean")
                nc.vector.tensor_scalar_mul(out=neg_mean[:], in0=z_sum_of[n][:], scalar1=-1.0 / PROJ)
                neg_mean_of[n] = neg_mean

        def apply_gain(n):
            m = n // GROUPS
            gained = work.tile([P, TILES, PROJ], F32, name="gained")
            for i in range(TILES):
                nc.vector.scalar_tensor_tensor(
                    out=gained[:, i, :], in0=z_of[n][:, i, :], scalar=neg_mean_of[n][:, i : i + 1],
                    in1=gamma_scaled[:, m, :], op0=ALU.add, op1=ALU.mult,
                )
            gained_of[n] = gained

        def square_sums(r):
            if r not in square_sums_of:
                sums = work.tile([P, 2 * TILES], F32, name="square_sums")
                square_sums_of[r] = sums
            return square_sums_of[r]

        def square_deviations(n):
            squares = work.tile([P, TILES, PROJ], F32, name="squares")
            dev_sum = square_sums(n + 1)[:, 0:TILES]
            for i in range(TILES):
                nc.scalar.activation(
                    out=squares[:, i, :], in_=z_of[n][:, i, :], func=ACT.Square,
                    bias=neg_mean_of[n][:, i : i + 1], scale=1.0, accum_out=dev_sum[:, i : i + 1],
                )

        def inverse_roots(n_std, n_norm):
            has_std, has_norm = 0 <= n_std < TOTAL, 0 <= n_norm < TOTAL
            if not (has_std or has_norm):
                return
            cols = slice(0 if has_std else TILES, 2 * TILES if has_norm else TILES)
            sums = square_sums_of[n_std + 1]
            radicands = work.tile([P, 2 * TILES], F32, name="radicands")
            roots = work.tile([P, 2 * TILES], F32, name="roots")
            nc.vector.scalar_tensor_tensor(
                out=radicands[:, cols], in0=sums[:, cols], scalar=NORM_EPS * NORM_EPS, in1=floors[:, cols],
                op0=ALU.max, op1=ALU.add,
            )
            nc.gpsimd.tensor_tensor(out=roots[:, cols], in0=radicands[:, cols], in1=minus_half[:, cols], op=ALU.pow)
            rstd_of[n_std] = roots[:, 0:TILES]
            inv_norm_of[n_norm] = roots[:, TILES : 2 * TILES]

        def shift(n):
            m = n // GROUPS
            y = work.tile([P, TILES, PROJ], F32, name="y")
            for i in range(TILES):
                nc.vector.scalar_tensor_tensor(
                    out=y[:, i, :], in0=gained_of[n][:, i, :], scalar=rstd_of[n][:, i : i + 1],
                    in1=beta_all[:, m, :], op0=ALU.mult, op1=ALU.add,
                )
            y_of[n] = y

        def square_y(n):
            y_squares = work.tile([P, TILES, PROJ], F32, name="y_squares")
            norm_sq = square_sums(n + 2)[:, TILES : 2 * TILES]
            for i in range(TILES):
                nc.scalar.activation(
                    out=y_squares[:, i, :], in_=y_of[n][:, i, :], func=ACT.Square, accum_out=norm_sq[:, i : i + 1]
                )

        def finish(n):
            m, g = divmod(n, GROUPS)
            result = work.tile([P, TILES, PROJ], F32, name="result")
            for i in range(TILES):
                nc.scalar.activation(
                    out=result[:, i, :], in_=y_of[n][:, i, :], func=ACT.Copy, scale=inv_norm_of[n][:, i : i + 1]
                )
            rows = out[m, GROUP * g : GROUP * (g + 1), :]
            nc.sync.dma_start(
                out=rows[0:VROWS].rearrange("(p i) c -> p i c", i=VTILES), in_=result[:, 0:VTILES, :]
            )
            nc.sync.dma_start(
                out=rows[VROWS:GROUP].rearrange("(i p) c -> p i c", p=P), in_=result[:, VTILES:TILES, :]
            )

        def run(stage, n, *args):
            if 0 <= n < TOTAL:
                stage(n, *args)

        for n in range(-2, TOTAL + 4):
            run(gelu, n, (0, 1, 2, 3))
            run(turn_pairs, n + 1)
            inverse_roots(n - 2, n - 3)
            run(add_bias, n - 1, (0, 1, 2, 3))
            if n >= 1:
                run(add_pairs, n + 2, 0)
            run(round_sums, n + 1, (0, 1))
            run(add_steps, n + 2)
            run(finish, n - 3)
            run(shift, n - 2)
            run(square_deviations, n - 1)
            run(quantise_pooled, n + 1)
            run(hidden, n + 1)
            run(group_h, n)
            run(square_y, n - 2)
            run(round_sums, n + 2, "tensor")
            run(apply_gain, n - 1)
            run(quantise_h, n)
            run(project, n)
            if n < 1:
                run(add_pairs, n + 2, 0)
            run(add_pairs, n + 2, 1)
            if n + 2 < MODS:
                regroup_w1(n + 2)
            if n == 0:
                nc.vector.tensor_scalar_mul(out=gamma_scaled[:], in0=gamma_all[:], scalar1=math.sqrt(PROJ))
            if n + 6 < TOTAL:
                load(n + 6)
